import numpy as np
import ml_dtypes


def mxq(x, axis, fmt="e4m3"):
    dtype, down = {"e4m3": (ml_dtypes.float8_e4m3fn, 7), "e5m2": (ml_dtypes.float8_e5m2, 14)}[fmt]
    v = np.moveaxis(np.asarray(x, np.float32).astype(ml_dtypes.bfloat16).astype(np.float64), axis, -1)
    blocks = v.reshape(v.shape[:-1] + (-1, 32))
    amax = np.abs(blocks).max(-1, keepdims=True)
    byte = np.maximum(np.where(amax > 0, np.frexp(amax)[1] - 1 + 127, 0) - down, 1)
    scale = np.exp2(byte - 127.0)
    codes = (blocks / scale).astype(np.float32).astype(dtype).astype(np.float64)
    return np.moveaxis((codes * scale).reshape(v.shape), -1, axis)


WIDE = False


def mx_kscale(k):
    if not WIDE:
        return np.ones(k)
    levels = np.array([10, -10, 5, -5, 0])
    a = np.random.permutation(np.resize(levels, k // 512 * 4)).reshape(k // 512, 4)
    idx = np.arange(k)
    return np.exp2(a[idx // 512, idx % 128 // 32])


BF16 = ml_dtypes.bfloat16


def bf(x):
    return np.asarray(x, np.float32).astype(BF16)


def f64(x):
    return np.asarray(x).astype(np.float64)


B, D, H = 256, 1024, 8192
HALF = D // 2


def setup_inputs():
    us, ut = mx_kscale(H), mx_kscale(H)
    return {
        "z": bf(np.random.standard_normal((B, D))),
        "W1_s": bf(np.random.standard_normal((HALF, H)) / np.sqrt(HALF) * us),
        "b1_s": bf(np.random.standard_normal(H) * 0.3 * us),
        "W2_s": bf(np.random.standard_normal((H, HALF)) * 0.5 / np.sqrt(H) / us[:, None]),
        "b2_s": bf(np.random.standard_normal(HALF) * 0.1),
        "W1_t": bf(np.random.standard_normal((HALF, H)) / np.sqrt(HALF) * ut),
        "b1_t": bf(np.random.standard_normal(H) * 0.3 * ut),
        "W2_t": bf(np.random.standard_normal((H, HALF)) / np.sqrt(H) / ut[:, None]),
        "b2_t": bf(np.random.standard_normal(HALF) * 0.3),
    }


def reference(z, W1_s, b1_s, W2_s, b2_s, W1_t, b1_t, W2_t, b2_t):
    z = f64(z)
    a = z[:, 0::2]
    b = z[:, 1::2]
    aq = mxq(a, 1, "e4m3")
    hs = np.maximum((aq @ mxq(f64(W1_s), 0, "e4m3")) + f64(b1_s), 0.0)
    s = (mxq(hs, 1, "e4m3") @ mxq(f64(W2_s), 0, "e4m3")) + f64(b2_s)
    ht = np.maximum((aq @ mxq(f64(W1_t), 0, "e4m3")) + f64(b1_t), 0.0)
    t = (mxq(ht, 1, "e4m3") @ mxq(f64(W2_t), 0, "e4m3")) + f64(b2_t)
    b_out = b * np.exp(s) + t
    logdet = s.sum(axis=1)
    z_out = np.stack([a, b_out], axis=2).reshape(B, D)
    return z_out, logdet

@@ -1,0 +1,317 @@
+from contextlib import ExitStack
+
+import concourse.mybir as mybir
+from concourse.masks import make_identity
+
+F32 = mybir.dt.float32
+BF16 = mybir.dt.bfloat16
+U32 = mybir.dt.uint32
+U8 = mybir.dt.uint8
+FP8X4 = mybir.dt.float8_e4m3fn_x4
+ACT = mybir.ActivationFunctionType
+ALU = mybir.AluOpType
+
+P = 128
+PACK = 4
+K_PASS = P * PACK
+ROWS, FEATURES, HIDDEN = 256, 1024, 8192
+HALF = FEATURES // 2
+ROW_TILES = ROWS // P
+NETS = 2
+PASSES = HIDDEN // K_PASS
+STEPS = NETS * PASSES
+RUN = 4
+AHEAD = 8
+DRAIN_TICKS = 2
+
+FLOPS = 2 * ROWS * HALF * HIDDEN * 2 * NETS
+
+
+def regroup(copy, grouped, planes):
+    copy(
+        out=grouped.rearrange("p (c i) t -> p c t i", i=RUN),
+        in_=planes.rearrange("p t (c i) -> p c t i", i=RUN),
+    )
+
+
+def tile_affinecoupling_pa_k_kernel(
+    tc, z, W1_s, b1_s, W2_s, b2_s, W1_t, b1_t, W2_t, b2_t, out_0, out_1
+):
+    nc = tc.nc
+    w1_dram = (W1_s, W1_t)
+    w2_dram = (W2_s, W2_t)
+
+    with ExitStack() as ctx:
+        ctx.enter_context(tc.manual_schedule())
+        const = ctx.enter_context(tc.tile_pool(name="const", bufs=1))
+        raw = ctx.enter_context(tc.tile_pool(name="raw", bufs=AHEAD))
+        work = ctx.enter_context(tc.tile_pool(name="work", bufs=4))
+        hidden_psum = ctx.enter_context(tc.psum_pool(name="hidden_psum", bufs=4))
+        sum_psum = ctx.enter_context(tc.psum_pool(name="sum_psum", bufs=NETS))
+
+        w1_raw, w2_raw = {}, {}
+        w1_grouped, w2_grouped, h_grouped = {}, {}, {}
+        w1_mx, w2_mx, h_mx = {}, {}, {}
+        h_banks, h_planes = {}, {}
+        sums = {}
+
+        def quantise(grouped, columns, name):
+            words = work.tile([P, columns], U32, name=name + "_words", align_bytes=64)
+            scales = work.tile([P, columns], U8, name=name + "_scales", align_bytes=64)
+            nc.vector.quantize_mx(
+                out=words[:].bitcast(FP8X4),
+                scales=scales[:],
+                in_=grouped[:].rearrange("p c t -> p (c t)"),
+            )
+            return words, scales
+
+
+        def load_w1(step):
+            if step >= STEPS:
+                return
+            net, g = divmod(step, PASSES)
+            w1_raw[step] = raw.tile([P, PACK, K_PASS], BF16, name="w1_raw")
+            units = slice(g * K_PASS, (g + 1) * K_PASS)
+            nc.sync.dma_start(
+                out=w1_raw[step][:],
+                in_=w1_dram[net][:, units].rearrange("(t p) h -> p t h", p=P),
+            )
+
+        def load_w2(step):
+            if step >= STEPS:
+                return
+            net, g = divmod(step, PASSES)
+            w2_raw[step] = raw.tile([P, PACK, HALF], BF16, name="w2_raw")
+            units = slice(g * K_PASS, (g + 1) * K_PASS)
+            nc.sync.dma_start(
+                out=w2_raw[step][:],
+                in_=w2_dram[net][units, :].rearrange("(t p) n -> p t n", p=P),
+            )
+
+        def regroup_w1(step):
+            if step >= STEPS:
+                return
+            w1_grouped[step] = work.tile(
+                [P, K_PASS, PACK], BF16, name="w1_grouped", align_bytes=64
+            )
+            regroup(nc.vector.tensor_copy, w1_grouped[step][:], w1_raw[step][:])
+
+        def regroup_w2(step):
+            if step >= STEPS:
+                return
+            w2_grouped[step] = work.tile(
+                [P, HALF, PACK], BF16, name="w2_grouped", align_bytes=64
+            )
+            regroup(nc.scalar.copy, w2_grouped[step][:], w2_raw[step][:])
+
+        def quantise_w1(step):
+            if step >= STEPS:
+                return
+            w1_mx[step] = quantise(w1_grouped[step], K_PASS, "w1")
+
+        def quantise_w2(step):
+            if step >= STEPS:
+                return
+            w2_mx[step] = quantise(w2_grouped[step], HALF, "w2")
+
+        def first_matmul(step):
+            if step >= STEPS:
+                return
+            words, scales = w1_mx[step]
+            h_banks[step] = []
+            for pair in range(PACK // 2):
+                bank = hidden_psum.tile([P, 2, ROWS], F32, name="h_bank")
+                h_banks[step].append(bank)
+                for i in range(2):
+                    t = 2 * pair + i
+                    units = slice(t * P, (t + 1) * P)
+                    nc.tensor.matmul_mx(
+                        out=bank[:, i, :],
+                        lhsT=words[:, units].bitcast(FP8X4),
+                        lhsT_scale=scales[:, units],
+                        rhs=a_words[:].bitcast(FP8X4),
+                        rhs_scale=a_scales[:],
+                        start=True,
+                        stop=True,
+                    )
+
+        def bias_relu(step):
+            if not 0 <= step < STEPS:
+                return
+            h_planes[step] = work.tile([P, PACK, ROWS], BF16, name="h_planes")
+            for t in range(PACK):
+                nc.scalar.activation(
+                    out=h_planes[step][:, t, :],
+                    in_=h_banks[step][t // 2][:, t % 2, :],
+                    func=ACT.Relu,
+                    bias=b1_columns[:, step * PACK + t : step * PACK + t + 1],
+                    scale=1.0,
+                )
+
+        def regroup_h(step):
+            if not 0 <= step < STEPS:
+                return
+            h_grouped[step] = work.tile([P, ROWS, PACK], BF16, name="h_grouped", align_bytes=64)
+            regroup(nc.vector.tensor_copy, h_grouped[step][:], h_planes[step][:])
+
+        def quantise_h(step):
+            if not 0 <= step < STEPS:
+                return
+            h_mx[step] = quantise(h_grouped[step], ROWS, "h")
+
+        def second_matmul(step):
+            if not 0 <= step < STEPS:
+                return
+            net, g = divmod(step, PASSES)
+            if g == 0:
+                sums[net] = [
+                    sum_psum.tile([P, HALF], F32, name="sum%d" % r) for r in range(ROW_TILES)
+                ]
+            h_words, h_scales = h_mx[step]
+            w_words, w_scales = w2_mx[step]
+            for r in range(ROW_TILES):
+                rows = slice(r * P, (r + 1) * P)
+                nc.tensor.matmul_mx(
+                    out=sums[net][r][:],
+                    lhsT=h_words[:, rows].bitcast(FP8X4),
+                    lhsT_scale=h_scales[:, rows],
+                    rhs=w_words[:].bitcast(FP8X4),
+                    rhs_scale=w_scales[:],
+                    start=(g == 0),
+                    stop=(g == PASSES - 1),
+                )
+
+
+        def s_bias_and_row_sum(step):
+            if step != PASSES - 1:
+                return
+            for r in range(ROW_TILES):
+                nc.vector.scalar_tensor_tensor(
+                    out=s_sb[:, r, :],
+                    in0=sums[0][r][:],
+                    scalar=1.0,
+                    in1=b2_s_rows[:],
+                    op0=ALU.mult,
+                    op1=ALU.add,
+                    accum_out=logdet_columns[:, r : r + 1],
+                )
+
+        def logdet_transpose(step):
+            if step != PASSES - 1:
+                return
+            logdet_psum = sum_psum.tile([P, P], F32, name="logdet_psum", tag="sum0")
+            sums["logdet"] = logdet_psum
+            nc.tensor.transpose(out=logdet_psum[:], in_=logdet_columns[:], identity=identity_f32[:])
+
+        def s_exp(step):
+            if step != PASSES - 1:
+                return
+            for r in range(ROW_TILES):
+                nc.scalar.activation(out=shift[:, r, :], in_=s_sb[:, r, :], func=ACT.Exp)
+            nc.scalar.copy(out=logdet_rows[:], in_=sums["logdet"][:])
+
+        def s_combine(step):
+            if step != PASSES - 1:
+                return
+            for r in range(ROW_TILES):
+                nc.vector.tensor_tensor(
+                    out=shift[:, r, :], in0=shift[:, r, :], in1=z_pairs[:, r, :, 1], op=ALU.mult
+                )
+            for r in range(ROW_TILES):
+                nc.vector.tensor_tensor(
+                    out=shift[:, r, :], in0=shift[:, r, :], in1=b2_t_rows[:], op=ALU.add
+                )
+
+
+        z_sb = const.tile([P, ROW_TILES, FEATURES], BF16)
+        b1_rows = const.tile([P, P], BF16)
+        load_w2(0)
+        nc.sync.dma_start(out=z_sb[:], in_=z.rearrange("(r p) d -> p r d", p=P))
+        load_w1(0)
+        nc.sync.dma_start(out=b1_rows[0 : P // 2, :], in_=b1_s.rearrange("(i c) -> i c", c=P))
+        nc.sync.dma_start(out=b1_rows[P // 2 : P, :], in_=b1_t.rearrange("(i c) -> i c", c=P))
+        for step in range(1, AHEAD):
+            load_w2(step)
+            load_w1(step)
+        b2_s_rows = const.tile([P, HALF], BF16)
+        b2_t_rows = const.tile([P, HALF], BF16)
+        nc.sync.dma_start(out=b2_s_rows[:], in_=b2_s.partition_broadcast(P))
+        nc.sync.dma_start(out=b2_t_rows[:], in_=b2_t.partition_broadcast(P))
+
+        identity_bf16 = const.tile([P, P], BF16)
+        identity_f32 = const.tile([P, P], F32)
+        make_identity(nc, identity_bf16[:])
+        make_identity(nc, identity_f32[:])
+
+        table_in = const.tile([P, 1], F32)
+        table_out = const.tile([P, 1], F32)
+        nc.vector.memset(table_in[:], 0.0)
+        nc.scalar.activation(out=table_out[:], in_=table_in[:], func=ACT.Exp)
+
+        logdet_columns = const.tile([P, P], F32)
+        logdet_rows = const.tile([P, P], F32)
+        nc.vector.memset(logdet_columns[:], 0.0)
+        s_sb = const.tile([P, ROW_TILES, HALF], F32)
+        shift = const.tile([P, ROW_TILES, HALF], F32)
+
+        regroup_w2(0)
+
+        z_pairs = z_sb[:].rearrange("p r (k e) -> p r k e", e=2)
+        a_sb = const.tile([P, ROW_TILES, HALF], BF16)
+        nc.vector.tensor_copy(out=a_sb[:], in_=z_pairs[:, :, :, 0])
+        a_psum = hidden_psum.tile([P, ROW_TILES, PACK, P], BF16, name="a_psum", tag="h_bank")
+        for r in range(ROW_TILES):
+            for t in range(PACK):
+                nc.tensor.transpose(
+                    out=a_psum[:, r, t, :],
+                    in_=a_sb[:, r, t * P : (t + 1) * P],
+                    identity=identity_bf16[:],
+                )
+        a_grouped = const.tile([P, ROWS, PACK], BF16, align_bytes=64)
+        nc.vector.tensor_copy(
+            out=a_grouped[:].rearrange("p (r i) t -> p r i t", r=ROW_TILES),
+            in_=a_psum[:].rearrange("p r t i -> p r i t"),
+        )
+
+        z_out_sb = const.tile([P, ROW_TILES, FEATURES], F32)
+        nc.vector.tensor_copy(out=z_out_sb[:], in_=z_sb[:])
+
+        a_words = const.tile([P, ROWS], U32, align_bytes=64)
+        a_scales = const.tile([P, ROWS], U8, align_bytes=64)
+        nc.vector.quantize_mx(
+            out=a_words[:].bitcast(FP8X4),
+            scales=a_scales[:],
+            in_=a_grouped[:].rearrange("p c t -> p (c t)"),
+        )
+
+        b1_psum = hidden_psum.tile([P, P], BF16, name="b1_psum", tag="h_bank")
+        nc.tensor.transpose(out=b1_psum[:], in_=b1_rows[:], identity=identity_bf16[:])
+        b1_columns = const.tile([P, P], F32)
+        nc.vector.tensor_copy(out=b1_columns[:], in_=b1_psum[:])
+
+        for tick in range(STEPS + DRAIN_TICKS):
+            logdet_transpose(tick - 4)
+            regroup_w2(tick + 1)
+            regroup_w1(tick)
+            bias_relu(tick - 1)
+            quantise_w2(tick)
+            regroup_h(tick - 2)
+            quantise_w1(tick)
+            first_matmul(tick)
+            quantise_h(tick - 2)
+            second_matmul(tick - 2)
+            s_exp(tick - 4)
+            s_bias_and_row_sum(tick - 3)
+            s_combine(tick - 5)
+            load_w2(tick + AHEAD)
+            load_w1(tick + AHEAD)
+
+        nc.sync.dma_start(
+            out=out_1.rearrange("(r i) -> r i", r=ROW_TILES), in_=logdet_rows[0:ROW_TILES, :]
+        )
+        z_out_pairs = z_out_sb[:].rearrange("p r (k e) -> p r k e", e=2)
+        for r in range(ROW_TILES):
+            nc.vector.tensor_tensor(
+                out=z_out_pairs[:, r, :, 1], in0=sums[1][r][:], in1=shift[:, r, :], op=ALU.add
+            )
+            nc.sync.dma_start(out=out_0[r * P : (r + 1) * P, :], in_=z_out_sb[:, r, :])

@@ -53,6 +53,7 @@ def tile_affinecoupling_pa_k_kernel(
         w1_grouped, w2_grouped, h_grouped = {}, {}, {}
         w1_mx, w2_mx, h_mx = {}, {}, {}
         h_banks, h_planes = {}, {}
+        second_biases = {}
         sums = {}
 
         def quantise(grouped, columns, name):
@@ -182,19 +183,37 @@ def tile_affinecoupling_pa_k_kernel(
                 )
 
 
-        def s_bias_and_row_sum(step):
+        def s_bias_and_row_sum(step, r):
             if step != PASSES - 1:
                 return
-            for r in range(ROW_TILES):
-                nc.vector.scalar_tensor_tensor(
-                    out=s_sb[:, r, :],
-                    in0=sums[0][r][:],
-                    scalar=1.0,
-                    in1=b2_s_rows[:],
-                    op0=ALU.mult,
-                    op1=ALU.add,
-                    accum_out=logdet_columns[:, r : r + 1],
-                )
+            nc.vector.scalar_tensor_tensor(
+                out=s_sb[:, r, :],
+                in0=sums[0][r][:],
+                scalar=1.0,
+                in1=second_biases["s"][:],
+                op0=ALU.mult,
+                op1=ALU.add,
+                accum_out=logdet_columns[:, r : r + 1],
+            )
+
+        def s_exp(step, r):
+            if step != PASSES - 1:
+                return
+            nc.scalar.activation(out=shift[:, r, :], in_=s_sb[:, r, :], func=ACT.Exp)
+
+        def s_times_b(step, r):
+            if step != PASSES - 1:
+                return
+            nc.vector.tensor_tensor(
+                out=shift[:, r, :], in0=shift[:, r, :], in1=z_pairs[:, r, :, 1], op=ALU.mult
+            )
+
+        def s_plus_bias(step, r):
+            if step != PASSES - 1:
+                return
+            nc.vector.tensor_tensor(
+                out=shift[:, r, :], in0=shift[:, r, :], in1=second_biases["t"][:], op=ALU.add
+            )
 
         def logdet_transpose(step):
             if step != PASSES - 1:
@@ -203,24 +222,22 @@ def tile_affinecoupling_pa_k_kernel(
             sums["logdet"] = logdet_psum
             nc.tensor.transpose(out=logdet_psum[:], in_=logdet_columns[:], identity=identity_f32[:])
 
-        def s_exp(step):
+        def logdet_copy(step):
             if step != PASSES - 1:
                 return
-            for r in range(ROW_TILES):
-                nc.scalar.activation(out=shift[:, r, :], in_=s_sb[:, r, :], func=ACT.Exp)
             nc.scalar.copy(out=logdet_rows[:], in_=sums["logdet"][:])
 
-        def s_combine(step):
-            if step != PASSES - 1:
+        def load_second_biases(step):
+            if step != PASSES // 2:
                 return
-            for r in range(ROW_TILES):
-                nc.vector.tensor_tensor(
-                    out=shift[:, r, :], in0=shift[:, r, :], in1=z_pairs[:, r, :, 1], op=ALU.mult
-                )
-            for r in range(ROW_TILES):
-                nc.vector.tensor_tensor(
-                    out=shift[:, r, :], in0=shift[:, r, :], in1=b2_t_rows[:], op=ALU.add
-                )
+            for net_name, bias in (("s", b2_s), ("t", b2_t)):
+                second_biases[net_name] = const.tile([P, HALF], BF16, name="b2_" + net_name)
+                nc.sync.dma_start(out=second_biases[net_name][:], in_=bias.partition_broadcast(P))
+
+        def start_z_out(step):
+            if step != STEPS - 1:
+                return
+            nc.vector.tensor_copy(out=z_out_sb[:], in_=z_sb[:])
 
 
         z_sb = const.tile([P, ROW_TILES, FEATURES], BF16)
@@ -233,10 +250,6 @@ def tile_affinecoupling_pa_k_kernel(
         for step in range(1, AHEAD):
             load_w2(step)
             load_w1(step)
-        b2_s_rows = const.tile([P, HALF], BF16)
-        b2_t_rows = const.tile([P, HALF], BF16)
-        nc.sync.dma_start(out=b2_s_rows[:], in_=b2_s.partition_broadcast(P))
-        nc.sync.dma_start(out=b2_t_rows[:], in_=b2_t.partition_broadcast(P))
 
         identity_bf16 = const.tile([P, P], BF16)
         identity_f32 = const.tile([P, P], F32)
@@ -267,14 +280,17 @@ def tile_affinecoupling_pa_k_kernel(
                     in_=a_sb[:, r, t * P : (t + 1) * P],
                     identity=identity_bf16[:],
                 )
+        regroup_w1(0)
         a_grouped = const.tile([P, ROWS, PACK], BF16, align_bytes=64)
         nc.vector.tensor_copy(
             out=a_grouped[:].rearrange("p (r i) t -> p r i t", r=ROW_TILES),
             in_=a_psum[:].rearrange("p r t i -> p r i t"),
         )
 
-        z_out_sb = const.tile([P, ROW_TILES, FEATURES], F32)
-        nc.vector.tensor_copy(out=z_out_sb[:], in_=z_sb[:])
+        b1_psum = hidden_psum.tile([P, P], BF16, name="b1_psum", tag="h_bank")
+        nc.tensor.transpose(out=b1_psum[:], in_=b1_rows[:], identity=identity_bf16[:])
+        b1_columns = const.tile([P, P], F32)
+        nc.vector.tensor_copy(out=b1_columns[:], in_=b1_psum[:])
 
         a_words = const.tile([P, ROWS], U32, align_bytes=64)
         a_scales = const.tile([P, ROWS], U8, align_bytes=64)
@@ -284,15 +300,12 @@ def tile_affinecoupling_pa_k_kernel(
             in_=a_grouped[:].rearrange("p c t -> p (c t)"),
         )
 
-        b1_psum = hidden_psum.tile([P, P], BF16, name="b1_psum", tag="h_bank")
-        nc.tensor.transpose(out=b1_psum[:], in_=b1_rows[:], identity=identity_bf16[:])
-        b1_columns = const.tile([P, P], F32)
-        nc.vector.tensor_copy(out=b1_columns[:], in_=b1_psum[:])
+        z_out_sb = const.tile([P, ROW_TILES, FEATURES], F32)
 
         for tick in range(STEPS + DRAIN_TICKS):
-            logdet_transpose(tick - 4)
+            logdet_transpose(tick - 5)
             regroup_w2(tick + 1)
-            regroup_w1(tick)
+            regroup_w1(tick + 1)
             bias_relu(tick - 1)
             quantise_w2(tick)
             regroup_h(tick - 2)
@@ -300,9 +313,14 @@ def tile_affinecoupling_pa_k_kernel(
             first_matmul(tick)
             quantise_h(tick - 2)
             second_matmul(tick - 2)
-            s_exp(tick - 4)
-            s_bias_and_row_sum(tick - 3)
-            s_combine(tick - 5)
+            start_z_out(tick - 1)
+            for r in range(ROW_TILES):
+                s_bias_and_row_sum(tick - 3 - r, r)
+                s_exp(tick - 4 - r, r)
+                s_times_b(tick - 5 - r, r)
+                s_plus_bias(tick - 7 - r, r)
+            logdet_copy(tick - 6)
+            load_second_biases(tick)
             load_w2(tick + AHEAD)
             load_w1(tick + AHEAD)
 

@@ -19,10 +19,10 @@ HALF = FEATURES // 2
 ROW_TILES = ROWS // P
 NETS = 2
 PASSES = HIDDEN // K_PASS
-STEPS = NETS * PASSES
 RUN = 4
-AHEAD = 8
-DRAIN_TICKS = 2
+GROUP_SIZES = ((1, 1, 2, 2, 2, 2, 2, 2, 2), (2, 2, 2, 2, 2, 2, 2, 1, 1))
+LAG = 2
+LOADS_AHEAD = 4
 
 FLOPS = 2 * ROWS * HALF * HIDDEN * 2 * NETS
 
@@ -41,91 +41,112 @@ def tile_affinecoupling_pa_k_kernel(
     w1_dram = (W1_s, W1_t)
     w2_dram = (W2_s, W2_t)
 
+    groups = []
+    for net in range(NETS):
+        first = 0
+        for size in GROUP_SIZES[net]:
+            groups.append((net, first, size))
+            first += size
+    n_groups = len(groups)
+    last_of_s = len(GROUP_SIZES[0]) - 1
+
+    def steps_in(j):
+        return groups[j][2] if 0 <= j < n_groups else 0
+
+    def w1_columns(j):
+        return K_PASS * steps_in(j)
+
+    def x_columns(j):
+        return w1_columns(j) + ROWS * steps_in(j - LAG)
+
     with ExitStack() as ctx:
         ctx.enter_context(tc.manual_schedule())
         const = ctx.enter_context(tc.tile_pool(name="const", bufs=1))
-        raw = ctx.enter_context(tc.tile_pool(name="raw", bufs=AHEAD))
-        work = ctx.enter_context(tc.tile_pool(name="work", bufs=4))
+        raw = ctx.enter_context(tc.tile_pool(name="raw", bufs=LOADS_AHEAD))
+        short = ctx.enter_context(tc.tile_pool(name="short", bufs=2))
+        work = ctx.enter_context(tc.tile_pool(name="work", bufs=3))
         hidden_psum = ctx.enter_context(tc.psum_pool(name="hidden_psum", bufs=4))
         sum_psum = ctx.enter_context(tc.psum_pool(name="sum_psum", bufs=NETS))
 
-        w1_raw, w2_raw = {}, {}
-        w1_grouped, w2_grouped, h_grouped = {}, {}, {}
+        x_planes, w2_planes = {}, {}
+        x_grouped, w2_grouped = {}, {}
         w1_mx, w2_mx, h_mx = {}, {}, {}
-        h_banks, h_planes = {}, {}
+        h_banks = {}
         second_biases = {}
         sums = {}
 
-        def quantise(grouped, columns, name):
-            words = work.tile([P, columns], U32, name=name + "_words", align_bytes=64)
-            scales = work.tile([P, columns], U8, name=name + "_scales", align_bytes=64)
+        def quantise(pool, grouped, columns, name):
+            words = pool.tile([P, columns], U32, name=name + "_words", align_bytes=64)
+            scales = pool.tile([P, columns], U8, name=name + "_scales", align_bytes=64)
             nc.vector.quantize_mx(
                 out=words[:].bitcast(FP8X4),
                 scales=scales[:],
-                in_=grouped[:].rearrange("p c t -> p (c t)"),
+                in_=grouped.rearrange("p c t -> p (c t)"),
             )
             return words, scales
 
 
-        def load_w1(step):
-            if step >= STEPS:
+        def load_x(j):
+            if x_columns(j) == 0:
                 return
-            net, g = divmod(step, PASSES)
-            w1_raw[step] = raw.tile([P, PACK, K_PASS], BF16, name="w1_raw")
-            units = slice(g * K_PASS, (g + 1) * K_PASS)
+            x_planes[j] = raw.tile([P, PACK, x_columns(j)], BF16, name="x_planes")
+            if steps_in(j) == 0:
+                return
+            net, first, size = groups[j]
+            units = slice(first * K_PASS, (first + size) * K_PASS)
             nc.sync.dma_start(
-                out=w1_raw[step][:],
+                out=x_planes[j][:, :, 0 : w1_columns(j)],
                 in_=w1_dram[net][:, units].rearrange("(t p) h -> p t h", p=P),
             )
 
-        def load_w2(step):
-            if step >= STEPS:
+        def load_w2(j):
+            if steps_in(j) == 0:
                 return
-            net, g = divmod(step, PASSES)
-            w2_raw[step] = raw.tile([P, PACK, HALF], BF16, name="w2_raw")
-            units = slice(g * K_PASS, (g + 1) * K_PASS)
-            nc.sync.dma_start(
-                out=w2_raw[step][:],
-                in_=w2_dram[net][units, :].rearrange("(t p) n -> p t n", p=P),
+            net, first, size = groups[j]
+            w2_planes[j] = raw.tile([P, PACK, size * HALF], BF16, name="w2_planes")
+            for g in range(size):
+                units = slice((first + g) * K_PASS, (first + g + 1) * K_PASS)
+                nc.sync.dma_start(
+                    out=w2_planes[j][:, :, g * HALF : (g + 1) * HALF],
+                    in_=w2_dram[net][units, :].rearrange("(t p) n -> p t n", p=P),
+                )
+
+        def regroup_x(j):
+            if x_columns(j) == 0:
+                return
+            x_grouped[j] = short.tile(
+                [P, x_columns(j), PACK], BF16, name="x_grouped", align_bytes=64
             )
+            regroup(nc.vector.tensor_copy, x_grouped[j][:], x_planes[j][:])
 
-        def regroup_w1(step):
-            if step >= STEPS:
+        def regroup_w2(j):
+            if steps_in(j) == 0:
                 return
-            w1_grouped[step] = work.tile(
-                [P, K_PASS, PACK], BF16, name="w1_grouped", align_bytes=64
+            w2_grouped[j] = work.tile(
+                [P, steps_in(j) * HALF, PACK], BF16, name="w2_grouped", align_bytes=64
             )
-            regroup(nc.vector.tensor_copy, w1_grouped[step][:], w1_raw[step][:])
+            regroup(nc.scalar.copy, w2_grouped[j][:], w2_planes[j][:])
 
-        def regroup_w2(step):
-            if step >= STEPS:
+        def quantise_w1(j):
+            if steps_in(j) == 0:
                 return
-            w2_grouped[step] = work.tile(
-                [P, HALF, PACK], BF16, name="w2_grouped", align_bytes=64
-            )
-            regroup(nc.scalar.copy, w2_grouped[step][:], w2_raw[step][:])
+            w1_mx[j] = quantise(short, x_grouped[j][:, 0 : w1_columns(j), :], w1_columns(j), "w1")
 
-        def quantise_w1(step):
-            if step >= STEPS:
+        def quantise_w2(j):
+            if steps_in(j) == 0:
                 return
-            w1_mx[step] = quantise(w1_grouped[step], K_PASS, "w1")
+            w2_mx[j] = quantise(work, w2_grouped[j][:], steps_in(j) * HALF, "w2")
 
-        def quantise_w2(step):
-            if step >= STEPS:
+        def first_matmul(j):
+            if steps_in(j) == 0:
                 return
-            w2_mx[step] = quantise(w2_grouped[step], HALF, "w2")
-
-        def first_matmul(step):
-            if step >= STEPS:
-                return
-            words, scales = w1_mx[step]
-            h_banks[step] = []
-            for pair in range(PACK // 2):
+            words, scales = w1_mx[j]
+            h_banks[j] = []
+            for half_step in range(steps_in(j) * PACK // 2):
                 bank = hidden_psum.tile([P, 2, ROWS], F32, name="h_bank")
-                h_banks[step].append(bank)
+                h_banks[j].append(bank)
                 for i in range(2):
-                    t = 2 * pair + i
-                    units = slice(t * P, (t + 1) * P)
+                    units = slice((2 * half_step + i) * P, (2 * half_step + i + 1) * P)
                     nc.tensor.matmul_mx(
                         out=bank[:, i, :],
                         lhsT=words[:, units].bitcast(FP8X4),
@@ -136,56 +157,58 @@ def tile_affinecoupling_pa_k_kernel(
                         stop=True,
                     )
 
-        def bias_relu(step):
-            if not 0 <= step < STEPS:
+        def bias_relu(j):
+            if steps_in(j) == 0:
                 return
-            h_planes[step] = work.tile([P, PACK, ROWS], BF16, name="h_planes")
-            for t in range(PACK):
-                nc.scalar.activation(
-                    out=h_planes[step][:, t, :],
-                    in_=h_banks[step][t // 2][:, t % 2, :],
-                    func=ACT.Relu,
-                    bias=b1_columns[:, step * PACK + t : step * PACK + t + 1],
-                    scale=1.0,
+            net, first, size = groups[j]
+            for g in range(size):
+                rows = slice(
+                    w1_columns(j + LAG) + g * ROWS, w1_columns(j + LAG) + (g + 1) * ROWS
                 )
+                for t in range(PACK):
+                    tile_index = g * PACK + t
+                    bias_column = (net * PASSES + first) * PACK + tile_index
+                    nc.scalar.activation(
+                        out=x_planes[j + LAG][:, t, rows],
+                        in_=h_banks[j][tile_index // 2][:, tile_index % 2, :],
+                        func=ACT.Relu,
+                        bias=b1_columns[:, bias_column : bias_column + 1],
+                        scale=1.0,
+                    )
 
-        def regroup_h(step):
-            if not 0 <= step < STEPS:
+        def quantise_h(j):
+            if steps_in(j) == 0:
                 return
-            h_grouped[step] = work.tile([P, ROWS, PACK], BF16, name="h_grouped", align_bytes=64)
-            regroup(nc.vector.tensor_copy, h_grouped[step][:], h_planes[step][:])
+            h_mx[j] = quantise(
+                short, x_grouped[j + LAG][:, w1_columns(j + LAG) :, :], steps_in(j) * ROWS, "h"
+            )
 
-        def quantise_h(step):
-            if not 0 <= step < STEPS:
+        def second_matmul(j):
+            if steps_in(j) == 0:
                 return
-            h_mx[step] = quantise(h_grouped[step], ROWS, "h")
-
-        def second_matmul(step):
-            if not 0 <= step < STEPS:
-                return
-            net, g = divmod(step, PASSES)
-            if g == 0:
+            net, first, size = groups[j]
+            if first == 0:
                 sums[net] = [
                     sum_psum.tile([P, HALF], F32, name="sum%d" % r) for r in range(ROW_TILES)
                 ]
-            h_words, h_scales = h_mx[step]
-            w_words, w_scales = w2_mx[step]
+            h_words, h_scales = h_mx[j]
+            w_words, w_scales = w2_mx[j]
             for r in range(ROW_TILES):
-                rows = slice(r * P, (r + 1) * P)
-                nc.tensor.matmul_mx(
-                    out=sums[net][r][:],
-                    lhsT=h_words[:, rows].bitcast(FP8X4),
-                    lhsT_scale=h_scales[:, rows],
-                    rhs=w_words[:].bitcast(FP8X4),
-                    rhs_scale=w_scales[:],
-                    start=(g == 0),
-                    stop=(g == PASSES - 1),
-                )
+                for g in range(size):
+                    rows = slice(g * ROWS + r * P, g * ROWS + (r + 1) * P)
+                    columns = slice(g * HALF, (g + 1) * HALF)
+                    nc.tensor.matmul_mx(
+                        out=sums[net][r][:],
+                        lhsT=h_words[:, rows].bitcast(FP8X4),
+                        lhsT_scale=h_scales[:, rows],
+                        rhs=w_words[:, columns].bitcast(FP8X4),
+                        rhs_scale=w_scales[:, columns],
+                        start=(first + g == 0),
+                        stop=(first + g == PASSES - 1),
+                    )
 
 
-        def s_bias_and_row_sum(step, r):
-            if step != PASSES - 1:
-                return
+        def s_bias_and_row_sum(r):
             nc.vector.scalar_tensor_tensor(
                 out=s_sb[:, r, :],
                 in0=sums[0][r][:],
@@ -196,60 +219,40 @@ def tile_affinecoupling_pa_k_kernel(
                 accum_out=logdet_columns[:, r : r + 1],
             )
 
-        def s_exp(step, r):
-            if step != PASSES - 1:
-                return
+        def s_exp(r):
             nc.scalar.activation(out=shift[:, r, :], in_=s_sb[:, r, :], func=ACT.Exp)
 
-        def s_times_b(step, r):
-            if step != PASSES - 1:
-                return
+        def s_times_b(r):
             nc.vector.tensor_tensor(
                 out=shift[:, r, :], in0=shift[:, r, :], in1=z_pairs[:, r, :, 1], op=ALU.mult
             )
 
-        def s_plus_bias(step, r):
-            if step != PASSES - 1:
-                return
+        def s_plus_bias(r):
             nc.vector.tensor_tensor(
                 out=shift[:, r, :], in0=shift[:, r, :], in1=second_biases["t"][:], op=ALU.add
             )
 
-        def logdet_transpose(step):
-            if step != PASSES - 1:
-                return
+        def logdet_transpose():
             logdet_psum = sum_psum.tile([P, P], F32, name="logdet_psum", tag="sum0")
             sums["logdet"] = logdet_psum
             nc.tensor.transpose(out=logdet_psum[:], in_=logdet_columns[:], identity=identity_f32[:])
 
-        def logdet_copy(step):
-            if step != PASSES - 1:
-                return
-            nc.scalar.copy(out=logdet_rows[:], in_=sums["logdet"][:])
-
-        def load_second_biases(step):
-            if step != PASSES // 2:
-                return
+        def load_second_biases():
             for net_name, bias in (("s", b2_s), ("t", b2_t)):
                 second_biases[net_name] = const.tile([P, HALF], BF16, name="b2_" + net_name)
                 nc.sync.dma_start(out=second_biases[net_name][:], in_=bias.partition_broadcast(P))
 
-        def start_z_out(step):
-            if step != STEPS - 1:
-                return
-            nc.vector.tensor_copy(out=z_out_sb[:], in_=z_sb[:])
-
 
         z_sb = const.tile([P, ROW_TILES, FEATURES], BF16)
         b1_rows = const.tile([P, P], BF16)
+        load_x(0)
         load_w2(0)
         nc.sync.dma_start(out=z_sb[:], in_=z.rearrange("(r p) d -> p r d", p=P))
-        load_w1(0)
         nc.sync.dma_start(out=b1_rows[0 : P // 2, :], in_=b1_s.rearrange("(i c) -> i c", c=P))
         nc.sync.dma_start(out=b1_rows[P // 2 : P, :], in_=b1_t.rearrange("(i c) -> i c", c=P))
-        for step in range(1, AHEAD):
-            load_w2(step)
-            load_w1(step)
+        for j in range(1, LOADS_AHEAD):
+            load_x(j)
+            load_w2(j)
 
         identity_bf16 = const.tile([P, P], BF16)
         identity_f32 = const.tile([P, P], F32)
@@ -266,63 +269,75 @@ def tile_affinecoupling_pa_k_kernel(
         nc.vector.memset(logdet_columns[:], 0.0)
         s_sb = const.tile([P, ROW_TILES, HALF], F32)
         shift = const.tile([P, ROW_TILES, HALF], F32)
-
-        regroup_w2(0)
-
+        z_out_sb = const.tile([P, ROW_TILES, FEATURES], F32)
         z_pairs = z_sb[:].rearrange("p r (k e) -> p r k e", e=2)
         a_sb = const.tile([P, ROW_TILES, HALF], BF16)
-        nc.vector.tensor_copy(out=a_sb[:], in_=z_pairs[:, :, :, 0])
-        a_psum = hidden_psum.tile([P, ROW_TILES, PACK, P], BF16, name="a_psum", tag="h_bank")
-        for r in range(ROW_TILES):
-            for t in range(PACK):
-                nc.tensor.transpose(
-                    out=a_psum[:, r, t, :],
-                    in_=a_sb[:, r, t * P : (t + 1) * P],
-                    identity=identity_bf16[:],
-                )
-        regroup_w1(0)
         a_grouped = const.tile([P, ROWS, PACK], BF16, align_bytes=64)
-        nc.vector.tensor_copy(
-            out=a_grouped[:].rearrange("p (r i) t -> p r i t", r=ROW_TILES),
-            in_=a_psum[:].rearrange("p r t i -> p r i t"),
-        )
-
-        b1_psum = hidden_psum.tile([P, P], BF16, name="b1_psum", tag="h_bank")
-        nc.tensor.transpose(out=b1_psum[:], in_=b1_rows[:], identity=identity_bf16[:])
         b1_columns = const.tile([P, P], F32)
-        nc.vector.tensor_copy(out=b1_columns[:], in_=b1_psum[:])
-
         a_words = const.tile([P, ROWS], U32, align_bytes=64)
         a_scales = const.tile([P, ROWS], U8, align_bytes=64)
-        nc.vector.quantize_mx(
-            out=a_words[:].bitcast(FP8X4),
-            scales=a_scales[:],
-            in_=a_grouped[:].rearrange("p c t -> p (c t)"),
-        )
+        head_psum = {}
 
-        z_out_sb = const.tile([P, ROW_TILES, FEATURES], F32)
-
-        for tick in range(STEPS + DRAIN_TICKS):
-            logdet_transpose(tick - 5)
-            regroup_w2(tick + 1)
-            regroup_w1(tick + 1)
-            bias_relu(tick - 1)
-            quantise_w2(tick)
-            regroup_h(tick - 2)
-            quantise_w1(tick)
-            first_matmul(tick)
-            quantise_h(tick - 2)
-            second_matmul(tick - 2)
-            start_z_out(tick - 1)
+        def transpose_a_and_b1():
+            nc.vector.tensor_copy(out=a_sb[:], in_=z_pairs[:, :, :, 0])
+            a_psum = hidden_psum.tile([P, ROW_TILES, PACK, P], BF16, name="a_psum", tag="h_bank")
             for r in range(ROW_TILES):
-                s_bias_and_row_sum(tick - 3 - r, r)
-                s_exp(tick - 4 - r, r)
-                s_times_b(tick - 5 - r, r)
-                s_plus_bias(tick - 7 - r, r)
-            logdet_copy(tick - 6)
-            load_second_biases(tick)
-            load_w2(tick + AHEAD)
-            load_w1(tick + AHEAD)
+                for t in range(PACK):
+                    nc.tensor.transpose(
+                        out=a_psum[:, r, t, :],
+                        in_=a_sb[:, r, t * P : (t + 1) * P],
+                        identity=identity_bf16[:],
+                    )
+            b1_psum = hidden_psum.tile([P, P], BF16, name="b1_psum", tag="h_bank")
+            nc.tensor.transpose(out=b1_psum[:], in_=b1_rows[:], identity=identity_bf16[:])
+            head_psum["a"] = a_psum
+            head_psum["b1"] = b1_psum
+
+        def quantise_a_and_copy_b1():
+            nc.vector.tensor_copy(
+                out=a_grouped[:].rearrange("p (r i) t -> p r i t", r=ROW_TILES),
+                in_=head_psum["a"][:].rearrange("p r t i -> p r i t"),
+            )
+            nc.vector.tensor_copy(out=b1_columns[:], in_=head_psum["b1"][:])
+            nc.vector.quantize_mx(
+                out=a_words[:].bitcast(FP8X4),
+                scales=a_scales[:],
+                in_=a_grouped[:].rearrange("p c t -> p (c t)"),
+            )
+
+        for tick in range(-LAG, n_groups):
+            since_s = tick - last_of_s
+            if since_s == 3:
+                logdet_transpose()
+            bias_relu(tick + 1)
+            regroup_w2(tick + 2)
+            regroup_x(tick + 2)
+            quantise_w2(tick + 1)
+            if tick == -LAG:
+                transpose_a_and_b1()
+            quantise_w1(tick + 2)
+            if tick == -LAG:
+                quantise_a_and_copy_b1()
+            first_matmul(tick + 2)
+            quantise_h(tick)
+            second_matmul(tick)
+            for r in range(ROW_TILES):
+                if since_s == 1 + r:
+                    s_bias_and_row_sum(r)
+                if since_s == 2 + r:
+                    s_exp(r)
+                if since_s == 3 + r:
+                    s_times_b(r)
+                if since_s == 5 + r:
+                    s_plus_bias(r)
+            if since_s == 4:
+                nc.scalar.copy(out=logdet_rows[:], in_=sums["logdet"][:])
+            if tick == n_groups - 2:
+                nc.scalar.copy(out=z_out_sb[:], in_=z_sb[:])
+            if tick == 2:
+                load_second_biases()
+            load_x(tick + 2 + LOADS_AHEAD)
+            load_w2(tick + 2 + LOADS_AHEAD)
 
         nc.sync.dma_start(
             out=out_1.rearrange("(r i) -> r i", r=ROW_TILES), in_=logdet_rows[0:ROW_TILES, :]

@@ -23,6 +23,9 @@ RUN = 4
 GROUP_SIZES = ((1, 1, 2, 2, 2, 2, 2, 2, 2), (2, 2, 2, 2, 2, 2, 2, 1, 1))
 LAG = 2
 LOADS_AHEAD = 4
+PE_COLUMNS = 192
+BANK_COLUMNS = 256
+MATMUL_COLUMNS = 128
 
 FLOPS = 2 * ROWS * HALF * HIDDEN * 2 * NETS
 
@@ -66,12 +69,13 @@ def tile_affinecoupling_pa_k_kernel(
         short = ctx.enter_context(tc.tile_pool(name="short", bufs=2))
         work = ctx.enter_context(tc.tile_pool(name="work", bufs=3))
         hidden_psum = ctx.enter_context(tc.psum_pool(name="hidden_psum", bufs=4))
-        sum_psum = ctx.enter_context(tc.psum_pool(name="sum_psum", bufs=NETS))
+        sum_psum = ctx.enter_context(tc.psum_pool(name="sum_psum", bufs=1))
+        w2_psum = ctx.enter_context(tc.psum_pool(name="w2_psum", bufs=2))
 
         x_planes, w2_planes = {}, {}
         x_grouped, w2_grouped = {}, {}
         w1_mx, w2_mx, h_mx = {}, {}, {}
-        h_banks = {}
+        h_banks, w2_banks = {}, {}
         second_biases = {}
         sums = {}
 
@@ -125,7 +129,35 @@ def tile_affinecoupling_pa_k_kernel(
             w2_grouped[j] = work.tile(
                 [P, steps_in(j) * HALF, PACK], BF16, name="w2_grouped", align_bytes=64
             )
-            regroup(nc.scalar.copy, w2_grouped[j][:], w2_planes[j][:])
+            by_tensor = steps_in(j) * PE_COLUMNS
+            regroup(
+                nc.scalar.copy, w2_grouped[j][:, by_tensor:, :], w2_planes[j][:, :, by_tensor:]
+            )
+            for b, bank in enumerate(w2_banks[j]):
+                columns = slice(b * BANK_COLUMNS, min((b + 1) * BANK_COLUMNS, by_tensor))
+                nc.scalar.copy(
+                    out=w2_grouped[j][:, columns, :],
+                    in_=bank[:, 0 : columns.stop - columns.start, :],
+                )
+
+        def regroup_w2_by_tensor(j):
+            if steps_in(j) == 0:
+                return
+            by_tensor = steps_in(j) * PE_COLUMNS
+            w2_banks[j] = []
+            for bank_start in range(0, by_tensor, BANK_COLUMNS):
+                bank = w2_psum.tile([P, BANK_COLUMNS, PACK], BF16, name="w2_bank")
+                w2_banks[j].append(bank)
+                bank_stop = min(bank_start + BANK_COLUMNS, by_tensor)
+                for start in range(bank_start, bank_stop, MATMUL_COLUMNS):
+                    stop = min(start + MATMUL_COLUMNS, bank_stop)
+                    nc.tensor.matmul(
+                        out=bank[:, start - bank_start : stop - bank_start, :],
+                        lhsT=identity_bf16[:],
+                        rhs=w2_planes[j][:, :, start:stop].rearrange("p t c -> p c t"),
+                        start=True,
+                        stop=True,
+                    )
 
         def quantise_w1(j):
             if steps_in(j) == 0:
@@ -233,7 +265,7 @@ def tile_affinecoupling_pa_k_kernel(
             )
 
         def logdet_transpose():
-            logdet_psum = sum_psum.tile([P, P], F32, name="logdet_psum", tag="sum0")
+            logdet_psum = hidden_psum.tile([P, P], F32, name="logdet_psum", tag="h_bank")
             sums["logdet"] = logdet_psum
             nc.tensor.transpose(out=logdet_psum[:], in_=logdet_columns[:], identity=identity_f32[:])
 
@@ -305,14 +337,21 @@ def tile_affinecoupling_pa_k_kernel(
                 in_=a_grouped[:].rearrange("p c t -> p (c t)"),
             )
 
+        regroup_w2_by_tensor(0)
+
         for tick in range(-LAG, n_groups):
             since_s = tick - last_of_s
+            bias_relu(tick + 1)
             if since_s == 3:
                 logdet_transpose()
-            bias_relu(tick + 1)
             regroup_w2(tick + 2)
+            if since_s == 3:
+                nc.scalar.copy(out=logdet_rows[:], in_=sums["logdet"][:])
             regroup_x(tick + 2)
             quantise_w2(tick + 1)
+            if since_s == 1:
+                for r in range(ROW_TILES):
+                    s_bias_and_row_sum(r)
             if tick == -LAG:
                 transpose_a_and_b1()
             quantise_w1(tick + 2)
@@ -321,17 +360,14 @@ def tile_affinecoupling_pa_k_kernel(
             first_matmul(tick + 2)
             quantise_h(tick)
             second_matmul(tick)
+            regroup_w2_by_tensor(tick + 3)
             for r in range(ROW_TILES):
-                if since_s == 1 + r:
-                    s_bias_and_row_sum(r)
                 if since_s == 2 + r:
                     s_exp(r)
                 if since_s == 3 + r:
                     s_times_b(r)
                 if since_s == 5 + r:
                     s_plus_bias(r)
-            if since_s == 4:
-                nc.scalar.copy(out=logdet_rows[:], in_=sums["logdet"][:])
             if tick == n_groups - 2:
                 nc.scalar.copy(out=z_out_sb[:], in_=z_sb[:])
             if tick == 2:

@@ -24,6 +24,7 @@ GROUP_SIZES = ((1, 1, 2, 2, 2, 2, 2, 2, 2), (2, 2, 2, 2, 2, 2, 2, 1, 1))
 LAG = 2
 LOADS_AHEAD = 4
 PE_COLUMNS = 192
+SCALAR_W1_COLUMNS = 32
 BANK_COLUMNS = 256
 MATMUL_COLUMNS = 128
 
@@ -115,13 +116,27 @@ def tile_affinecoupling_pa_k_kernel(
                     in_=w2_dram[net][units, :].rearrange("(t p) n -> p t n", p=P),
                 )
 
-        def regroup_x(j):
+        def regroup_x_by_scalar(j):
             if x_columns(j) == 0:
                 return
             x_grouped[j] = short.tile(
                 [P, x_columns(j), PACK], BF16, name="x_grouped", align_bytes=64
             )
-            regroup(nc.vector.tensor_copy, x_grouped[j][:], x_planes[j][:])
+            by_scalar = steps_in(j) * SCALAR_W1_COLUMNS
+            if by_scalar > 0:
+                regroup(
+                    nc.scalar.copy, x_grouped[j][:, 0:by_scalar, :], x_planes[j][:, :, 0:by_scalar]
+                )
+
+        def regroup_x(j):
+            if x_columns(j) == 0:
+                return
+            by_scalar = steps_in(j) * SCALAR_W1_COLUMNS
+            regroup(
+                nc.vector.tensor_copy,
+                x_grouped[j][:, by_scalar:, :],
+                x_planes[j][:, :, by_scalar:],
+            )
 
         def regroup_w2(j):
             if steps_in(j) == 0:
@@ -338,6 +353,7 @@ def tile_affinecoupling_pa_k_kernel(
             )
 
         regroup_w2_by_tensor(0)
+        regroup_x_by_scalar(0)
 
         for tick in range(-LAG, n_groups):
             since_s = tick - last_of_s
@@ -347,6 +363,7 @@ def tile_affinecoupling_pa_k_kernel(
             regroup_w2(tick + 2)
             if since_s == 3:
                 nc.scalar.copy(out=logdet_rows[:], in_=sums["logdet"][:])
+            regroup_x_by_scalar(tick + 3)
             regroup_x(tick + 2)
             quantise_w2(tick + 1)
             if since_s == 1:

@@ -316,6 +316,7 @@ def tile_affinecoupling_pa_k_kernel(
         nc.vector.memset(logdet_columns[:], 0.0)
         s_sb = const.tile([P, ROW_TILES, HALF], F32)
         shift = const.tile([P, ROW_TILES, HALF], F32)
+        z_out_planes = const.tile([P, ROW_TILES, 2, HALF], F32)
         z_out_sb = const.tile([P, ROW_TILES, FEATURES], F32)
         z_pairs = z_sb[:].rearrange("p r (k e) -> p r k e", e=2)
         a_sb = const.tile([P, ROW_TILES, HALF], BF16)
@@ -386,7 +387,7 @@ def tile_affinecoupling_pa_k_kernel(
                 if since_s == 5 + r:
                     s_plus_bias(r)
             if tick == n_groups - 2:
-                nc.scalar.copy(out=z_out_sb[:], in_=z_sb[:])
+                nc.scalar.copy(out=z_out_planes[:, :, 0, :], in_=a_sb[:])
             if tick == 2:
                 load_second_biases()
             load_x(tick + 2 + LOADS_AHEAD)
@@ -395,9 +396,13 @@ def tile_affinecoupling_pa_k_kernel(
         nc.sync.dma_start(
             out=out_1.rearrange("(r i) -> r i", r=ROW_TILES), in_=logdet_rows[0:ROW_TILES, :]
         )
-        z_out_pairs = z_out_sb[:].rearrange("p r (k e) -> p r k e", e=2)
         for r in range(ROW_TILES):
             nc.vector.tensor_tensor(
-                out=z_out_pairs[:, r, :, 1], in0=sums[1][r][:], in1=shift[:, r, :], op=ALU.add
+                out=z_out_planes[:, r, 1, :], in0=sums[1][r][:], in1=shift[:, r, :], op=ALU.add
+            )
+        for r, copy in enumerate((nc.scalar.copy, nc.vector.tensor_copy)):
+            copy(
+                out=z_out_sb[:, r, :].rearrange("p (k e) -> p k e", e=2),
+                in_=z_out_planes[:, r, :, :].rearrange("p e k -> p k e"),
             )
             nc.sync.dma_start(out=out_0[r * P : (r + 1) * P, :], in_=z_out_sb[:, r, :])

@@ -293,10 +293,10 @@ def tile_affinecoupling_pa_k_kernel(
         z_sb = const.tile([P, ROW_TILES, FEATURES], BF16)
         b1_rows = const.tile([P, P], BF16)
         load_x(0)
-        load_w2(0)
         nc.sync.dma_start(out=z_sb[:], in_=z.rearrange("(r p) d -> p r d", p=P))
         nc.sync.dma_start(out=b1_rows[0 : P // 2, :], in_=b1_s.rearrange("(i c) -> i c", c=P))
         nc.sync.dma_start(out=b1_rows[P // 2 : P, :], in_=b1_t.rearrange("(i c) -> i c", c=P))
+        load_w2(0)
         for j in range(1, LOADS_AHEAD):
             load_x(j)
             load_w2(j)
@@ -319,34 +319,28 @@ def tile_affinecoupling_pa_k_kernel(
         z_out_planes = const.tile([P, ROW_TILES, 2, HALF], F32)
         z_out_sb = const.tile([P, ROW_TILES, FEATURES], F32)
         z_pairs = z_sb[:].rearrange("p r (k e) -> p r k e", e=2)
-        a_sb = const.tile([P, ROW_TILES, HALF], BF16)
         a_grouped = const.tile([P, ROWS, PACK], BF16, align_bytes=64)
         b1_columns = const.tile([P, P], F32)
         a_words = const.tile([P, ROWS], U32, align_bytes=64)
         a_scales = const.tile([P, ROWS], U8, align_bytes=64)
-        head_psum = {}
 
-        def transpose_a_and_b1():
-            nc.vector.tensor_copy(out=a_sb[:], in_=z_pairs[:, :, :, 0])
-            a_psum = hidden_psum.tile([P, ROW_TILES, PACK, P], BF16, name="a_psum", tag="h_bank")
-            for r in range(ROW_TILES):
-                for t in range(PACK):
-                    nc.tensor.transpose(
-                        out=a_psum[:, r, t, :],
-                        in_=a_sb[:, r, t * P : (t + 1) * P],
-                        identity=identity_bf16[:],
-                    )
-            b1_psum = hidden_psum.tile([P, P], BF16, name="b1_psum", tag="h_bank")
-            nc.tensor.transpose(out=b1_psum[:], in_=b1_rows[:], identity=identity_bf16[:])
-            head_psum["a"] = a_psum
-            head_psum["b1"] = b1_psum
+        a_psum = hidden_psum.tile([P, ROW_TILES, PACK, P], BF16, name="a_psum", tag="h_bank")
+        for r in range(ROW_TILES):
+            for t in range(PACK):
+                nc.tensor.transpose(
+                    out=a_psum[:, r, t, :],
+                    in_=z_pairs[:, r, t * P : (t + 1) * P, 0],
+                    identity=identity_bf16[:],
+                )
+        b1_psum = hidden_psum.tile([P, P], BF16, name="b1_psum", tag="h_bank")
+        nc.tensor.transpose(out=b1_psum[:], in_=b1_rows[:], identity=identity_bf16[:])
 
         def quantise_a_and_copy_b1():
             nc.vector.tensor_copy(
                 out=a_grouped[:].rearrange("p (r i) t -> p r i t", r=ROW_TILES),
-                in_=head_psum["a"][:].rearrange("p r t i -> p r i t"),
+                in_=a_psum[:].rearrange("p r t i -> p r i t"),
             )
-            nc.vector.tensor_copy(out=b1_columns[:], in_=head_psum["b1"][:])
+            nc.vector.tensor_copy(out=b1_columns[:], in_=b1_psum[:])
             nc.vector.quantize_mx(
                 out=a_words[:].bitcast(FP8X4),
                 scales=a_scales[:],
@@ -355,6 +349,7 @@ def tile_affinecoupling_pa_k_kernel(
 
         regroup_w2_by_tensor(0)
         regroup_x_by_scalar(0)
+        nc.scalar.copy(out=z_out_planes[:, :, 0, :], in_=z_pairs[:, :, :, 0])
 
         for tick in range(-LAG, n_groups):
             since_s = tick - last_of_s
@@ -370,8 +365,6 @@ def tile_affinecoupling_pa_k_kernel(
             if since_s == 1:
                 for r in range(ROW_TILES):
                     s_bias_and_row_sum(r)
-            if tick == -LAG:
-                transpose_a_and_b1()
             quantise_w1(tick + 2)
             if tick == -LAG:
                 quantise_a_and_copy_b1()
@@ -386,8 +379,6 @@ def tile_affinecoupling_pa_k_kernel(
                     s_times_b(r)
                 if since_s == 5 + r:
                     s_plus_bias(r)
-            if tick == n_groups - 2:
-                nc.scalar.copy(out=z_out_planes[:, :, 0, :], in_=a_sb[:])
             if tick == 2:
                 load_second_biases()
             load_x(tick + 2 + LOADS_AHEAD)

@@ -20,11 +20,12 @@ ROW_TILES = ROWS // P
 NETS = 2
 PASSES = HIDDEN // K_PASS
 RUN = 4
-GROUP_SIZES = ((1, 1, 2, 2, 2, 2, 2, 2, 2), (2, 2, 2, 2, 2, 2, 2, 1, 1))
+GROUP_SIZES = ((1, 1, 1, 1, 2, 2, 2, 2, 2, 2), (2, 2, 2, 2, 2, 2, 2, 1, 1))
 LAG = 2
 LOADS_AHEAD = 4
 PE_COLUMNS = 192
 SCALAR_W1_COLUMNS = 32
+END_COLUMNS = 256
 BANK_COLUMNS = 256
 MATMUL_COLUMNS = 128
 
@@ -387,13 +388,22 @@ def tile_affinecoupling_pa_k_kernel(
         nc.sync.dma_start(
             out=out_1.rearrange("(r i) -> r i", r=ROW_TILES), in_=logdet_rows[0:ROW_TILES, :]
         )
+        pieces = [slice(k, k + END_COLUMNS) for k in range(0, HALF, END_COLUMNS)]
         for r in range(ROW_TILES):
-            nc.vector.tensor_tensor(
-                out=z_out_planes[:, r, 1, :], in0=sums[1][r][:], in1=shift[:, r, :], op=ALU.add
-            )
+            for piece in pieces:
+                nc.vector.tensor_tensor(
+                    out=z_out_planes[:, r, 1, piece],
+                    in0=sums[1][r][:, piece],
+                    in1=shift[:, r, piece],
+                    op=ALU.add,
+                )
         for r, copy in enumerate((nc.scalar.copy, nc.vector.tensor_copy)):
-            copy(
-                out=z_out_sb[:, r, :].rearrange("p (k e) -> p k e", e=2),
-                in_=z_out_planes[:, r, :, :].rearrange("p e k -> p k e"),
-            )
-            nc.sync.dma_start(out=out_0[r * P : (r + 1) * P, :], in_=z_out_sb[:, r, :])
+            for piece in pieces:
+                features = slice(2 * piece.start, 2 * piece.stop)
+                copy(
+                    out=z_out_sb[:, r, features].rearrange("p (k e) -> p k e", e=2),
+                    in_=z_out_planes[:, r, :, piece].rearrange("p e k -> p k e"),
+                )
+                nc.sync.dma_start(
+                    out=out_0[r * P : (r + 1) * P, features], in_=z_out_sb[:, r, features]
+                )

@@ -24,7 +24,7 @@ GROUP_SIZES = ((1, 1, 1, 1, 2, 2, 2, 2, 2, 2), (2, 2, 2, 2, 2, 2, 2, 1, 1))
 LAG = 2
 LOADS_AHEAD = 4
 PE_COLUMNS = 192
-SCALAR_W1_COLUMNS = 32
+SCALAR_W1_COLUMNS = 40
 END_COLUMNS = 256
 BANK_COLUMNS = 256
 MATMUL_COLUMNS = 128

@@ -19,12 +19,13 @@ HALF = FEATURES // 2
 ROW_TILES = ROWS // P
 NETS = 2
 PASSES = HIDDEN // K_PASS
-RUN = 4
+VECTOR_RUN = 8
+SCALAR_RUN = 4
 GROUP_SIZES = ((1, 1, 1, 1, 2, 2, 2, 2, 2, 2), (2, 2, 2, 2, 2, 2, 2, 1, 1))
 LAG = 2
 LOADS_AHEAD = 4
 PE_COLUMNS = 192
-SCALAR_W1_COLUMNS = 40
+SCALAR_W1_COLUMNS = 16
 END_COLUMNS = 256
 BANK_COLUMNS = 256
 MATMUL_COLUMNS = 128
@@ -32,10 +33,10 @@ MATMUL_COLUMNS = 128
 FLOPS = 2 * ROWS * HALF * HIDDEN * 2 * NETS
 
 
-def regroup(copy, grouped, planes):
+def regroup(copy, run, grouped, planes):
     copy(
-        out=grouped.rearrange("p (c i) t -> p c t i", i=RUN),
-        in_=planes.rearrange("p t (c i) -> p c t i", i=RUN),
+        out=grouped.rearrange("p (c i) t -> p c t i", i=run),
+        in_=planes.rearrange("p t (c i) -> p c t i", i=run),
     )
 
 
@@ -126,7 +127,7 @@ def tile_affinecoupling_pa_k_kernel(
             by_scalar = steps_in(j) * SCALAR_W1_COLUMNS
             if by_scalar > 0:
                 regroup(
-                    nc.scalar.copy, x_grouped[j][:, 0:by_scalar, :], x_planes[j][:, :, 0:by_scalar]
+                    nc.scalar.copy, SCALAR_RUN, x_grouped[j][:, 0:by_scalar, :], x_planes[j][:, :, 0:by_scalar]
                 )
 
         def regroup_x(j):
@@ -135,6 +136,7 @@ def tile_affinecoupling_pa_k_kernel(
             by_scalar = steps_in(j) * SCALAR_W1_COLUMNS
             regroup(
                 nc.vector.tensor_copy,
+                VECTOR_RUN,
                 x_grouped[j][:, by_scalar:, :],
                 x_planes[j][:, :, by_scalar:],
             )
@@ -147,7 +149,7 @@ def tile_affinecoupling_pa_k_kernel(
             )
             by_tensor = steps_in(j) * PE_COLUMNS
             regroup(
-                nc.scalar.copy, w2_grouped[j][:, by_tensor:, :], w2_planes[j][:, :, by_tensor:]
+                nc.scalar.copy, SCALAR_RUN, w2_grouped[j][:, by_tensor:, :], w2_planes[j][:, :, by_tensor:]
             )
             for b, bank in enumerate(w2_banks[j]):
                 columns = slice(b * BANK_COLUMNS, min((b + 1) * BANK_COLUMNS, by_tensor))

@@ -25,7 +25,7 @@ GROUP_SIZES = ((1, 1, 1, 1, 2, 2, 2, 2, 2, 2), (2, 2, 2, 2, 2, 2, 2, 1, 1))
 LAG = 2
 LOADS_AHEAD = 4
 PE_COLUMNS = 192
-SCALAR_W1_COLUMNS = 16
+SCALAR_W1_COLUMNS = 32
 END_COLUMNS = 256
 BANK_COLUMNS = 256
 MATMUL_COLUMNS = 128
@@ -382,7 +382,7 @@ def tile_affinecoupling_pa_k_kernel(
                     s_times_b(r)
                 if since_s == 5 + r:
                     s_plus_bias(r)
-            if tick == 2:
+            if tick == last_of_s - 3:
                 load_second_biases()
             load_x(tick + 2 + LOADS_AHEAD)
             load_w2(tick + 2 + LOADS_AHEAD)

@@ -20,11 +20,11 @@ ROW_TILES = ROWS // P
 NETS = 2
 PASSES = HIDDEN // K_PASS
 VECTOR_RUN = 8
-SCALAR_RUN = 4
+SCALAR_RUN = 8
 GROUP_SIZES = ((1, 1, 1, 1, 2, 2, 2, 2, 2, 2), (2, 2, 2, 2, 2, 2, 2, 1, 1))
 LAG = 2
 LOADS_AHEAD = 4
-PE_COLUMNS = 192
+PE_COLUMNS = 200
 SCALAR_W1_COLUMNS = 32
 END_COLUMNS = 256
 BANK_COLUMNS = 256
@@ -82,15 +82,20 @@ def tile_affinecoupling_pa_k_kernel(
         second_biases = {}
         sums = {}
 
-        def quantise(pool, grouped, columns, name):
+        def quantise(pool, grouped, columns, name, pieces=1):
             words = pool.tile([P, columns], U32, name=name + "_words", align_bytes=64)
             scales = pool.tile([P, columns], U8, name=name + "_scales", align_bytes=64)
-            nc.vector.quantize_mx(
-                out=words[:].bitcast(FP8X4),
-                scales=scales[:],
-                in_=grouped.rearrange("p c t -> p (c t)"),
-            )
+            for piece in range(pieces):
+                part = slice(piece * columns // pieces, (piece + 1) * columns // pieces)
+                nc.vector.quantize_mx(
+                    out=words[:, part].bitcast(FP8X4),
+                    scales=scales[:, part],
+                    in_=grouped[:, part, :].rearrange("p c t -> p (c t)"),
+                )
             return words, scales
+
+        def h_pieces(j):
+            return ROW_TILES if j == n_groups - 1 else 1
 
 
         def load_x(j):
@@ -134,12 +139,16 @@ def tile_affinecoupling_pa_k_kernel(
             if x_columns(j) == 0:
                 return
             by_scalar = steps_in(j) * SCALAR_W1_COLUMNS
-            regroup(
-                nc.vector.tensor_copy,
-                VECTOR_RUN,
-                x_grouped[j][:, by_scalar:, :],
-                x_planes[j][:, :, by_scalar:],
-            )
+            pieces = h_pieces(j - LAG)
+            width = (x_columns(j) - by_scalar) // pieces
+            for piece in range(pieces):
+                part = slice(by_scalar + piece * width, by_scalar + (piece + 1) * width)
+                regroup(
+                    nc.vector.tensor_copy,
+                    VECTOR_RUN,
+                    x_grouped[j][:, part, :],
+                    x_planes[j][:, :, part],
+                )
 
         def regroup_w2(j):
             if steps_in(j) == 0:
@@ -230,7 +239,11 @@ def tile_affinecoupling_pa_k_kernel(
             if steps_in(j) == 0:
                 return
             h_mx[j] = quantise(
-                short, x_grouped[j + LAG][:, w1_columns(j + LAG) :, :], steps_in(j) * ROWS, "h"
+                short,
+                x_grouped[j + LAG][:, w1_columns(j + LAG) :, :],
+                steps_in(j) * ROWS,
+                "h",
+                h_pieces(j),
             )
 
         def second_matmul(j):

@@ -82,16 +82,14 @@ def tile_affinecoupling_pa_k_kernel(
         second_biases = {}
         sums = {}
 
-        def quantise(pool, grouped, columns, name, pieces=1):
+        def quantise(pool, grouped, columns, name):
             words = pool.tile([P, columns], U32, name=name + "_words", align_bytes=64)
             scales = pool.tile([P, columns], U8, name=name + "_scales", align_bytes=64)
-            for piece in range(pieces):
-                part = slice(piece * columns // pieces, (piece + 1) * columns // pieces)
-                nc.vector.quantize_mx(
-                    out=words[:, part].bitcast(FP8X4),
-                    scales=scales[:, part],
-                    in_=grouped[:, part, :].rearrange("p c t -> p (c t)"),
-                )
+            nc.vector.quantize_mx(
+                out=words[:].bitcast(FP8X4),
+                scales=scales[:],
+                in_=grouped.rearrange("p c t -> p (c t)"),
+            )
             return words, scales
 
         def h_pieces(j):
@@ -138,17 +136,33 @@ def tile_affinecoupling_pa_k_kernel(
         def regroup_x(j):
             if x_columns(j) == 0:
                 return
-            by_scalar = steps_in(j) * SCALAR_W1_COLUMNS
-            pieces = h_pieces(j - LAG)
-            width = (x_columns(j) - by_scalar) // pieces
-            for piece in range(pieces):
-                part = slice(by_scalar + piece * width, by_scalar + (piece + 1) * width)
+            part = slice(steps_in(j) * SCALAR_W1_COLUMNS, x_columns(j))
+            regroup(
+                nc.vector.tensor_copy,
+                VECTOR_RUN,
+                x_grouped[j][:, part, :],
+                x_planes[j][:, :, part],
+            )
+
+        def last_hidden():
+            j = n_groups - 1
+            columns = steps_in(j) * ROWS
+            words = short.tile([P, columns], U32, name="h_words", align_bytes=64)
+            scales = short.tile([P, columns], U8, name="h_scales", align_bytes=64)
+            for r in range(ROW_TILES):
+                part = slice(r * P, (r + 1) * P)
                 regroup(
                     nc.vector.tensor_copy,
                     VECTOR_RUN,
-                    x_grouped[j][:, part, :],
-                    x_planes[j][:, :, part],
+                    x_grouped[j + LAG][:, part, :],
+                    x_planes[j + LAG][:, :, part],
                 )
+                nc.vector.quantize_mx(
+                    out=words[:, part].bitcast(FP8X4),
+                    scales=scales[:, part],
+                    in_=x_grouped[j + LAG][:, part, :].rearrange("p c t -> p (c t)"),
+                )
+            h_mx[j] = (words, scales)
 
         def regroup_w2(j):
             if steps_in(j) == 0:
@@ -224,16 +238,18 @@ def tile_affinecoupling_pa_k_kernel(
                 rows = slice(
                     w1_columns(j + LAG) + g * ROWS, w1_columns(j + LAG) + (g + 1) * ROWS
                 )
-                for t in range(PACK):
-                    tile_index = g * PACK + t
-                    bias_column = (net * PASSES + first) * PACK + tile_index
-                    nc.scalar.activation(
-                        out=x_planes[j + LAG][:, t, rows],
-                        in_=h_banks[j][tile_index // 2][:, tile_index % 2, :],
-                        func=ACT.Relu,
-                        bias=b1_columns[:, bias_column : bias_column + 1],
-                        scale=1.0,
-                    )
+                width = ROWS // h_pieces(j)
+                for start in range(0, ROWS, width):
+                    for t in range(PACK):
+                        tile_index = g * PACK + t
+                        bias_column = (net * PASSES + first) * PACK + tile_index
+                        nc.scalar.activation(
+                            out=x_planes[j + LAG][:, t, rows.start + start : rows.start + start + width],
+                            in_=h_banks[j][tile_index // 2][:, tile_index % 2, start : start + width],
+                            func=ACT.Relu,
+                            bias=b1_columns[:, bias_column : bias_column + 1],
+                            scale=1.0,
+                        )
 
         def quantise_h(j):
             if steps_in(j) == 0:
@@ -243,7 +259,6 @@ def tile_affinecoupling_pa_k_kernel(
                 x_grouped[j + LAG][:, w1_columns(j + LAG) :, :],
                 steps_in(j) * ROWS,
                 "h",
-                h_pieces(j),
             )
 
         def second_matmul(j):
@@ -376,7 +391,8 @@ def tile_affinecoupling_pa_k_kernel(
             if since_s == 3:
                 nc.scalar.copy(out=logdet_rows[:], in_=sums["logdet"][:])
             regroup_x_by_scalar(tick + 3)
-            regroup_x(tick + 2)
+            if tick < n_groups - 1:
+                regroup_x(tick + 2)
             quantise_w2(tick + 1)
             if since_s == 1:
                 for r in range(ROW_TILES):
@@ -385,7 +401,10 @@ def tile_affinecoupling_pa_k_kernel(
             if tick == -LAG:
                 quantise_a_and_copy_b1()
             first_matmul(tick + 2)
-            quantise_h(tick)
+            if tick < n_groups - 1:
+                quantise_h(tick)
+            else:
+                last_hidden()
             second_matmul(tick)
             regroup_w2_by_tensor(tick + 3)
             for r in range(ROW_TILES):
@@ -404,21 +423,27 @@ def tile_affinecoupling_pa_k_kernel(
             out=out_1.rearrange("(r i) -> r i", r=ROW_TILES), in_=logdet_rows[0:ROW_TILES, :]
         )
         pieces = [slice(k, k + END_COLUMNS) for k in range(0, HALF, END_COLUMNS)]
+
+        def add(r, piece):
+            nc.vector.tensor_tensor(
+                out=z_out_planes[:, r, 1, piece],
+                in0=sums[1][r][:, piece],
+                in1=shift[:, r, piece],
+                op=ALU.add,
+            )
+
+        def interleave_and_store(copy, r, piece):
+            features = slice(2 * piece.start, 2 * piece.stop)
+            copy(
+                out=z_out_sb[:, r, features].rearrange("p (k e) -> p k e", e=2),
+                in_=z_out_planes[:, r, :, piece].rearrange("p e k -> p k e"),
+            )
+            nc.sync.dma_start(
+                out=out_0[r * P : (r + 1) * P, features], in_=z_out_sb[:, r, features]
+            )
+
         for r in range(ROW_TILES):
             for piece in pieces:
-                nc.vector.tensor_tensor(
-                    out=z_out_planes[:, r, 1, piece],
-                    in0=sums[1][r][:, piece],
-                    in1=shift[:, r, piece],
-                    op=ALU.add,
-                )
-        for r, copy in enumerate((nc.scalar.copy, nc.vector.tensor_copy)):
-            for piece in pieces:
-                features = slice(2 * piece.start, 2 * piece.stop)
-                copy(
-                    out=z_out_sb[:, r, features].rearrange("p (k e) -> p k e", e=2),
-                    in_=z_out_planes[:, r, :, piece].rearrange("p e k -> p k e"),
-                )
-                nc.sync.dma_start(
-                    out=out_0[r * P : (r + 1) * P, features], in_=z_out_sb[:, r, features]
-                )
+                add(r, piece)
+            interleave_and_store(nc.vector.tensor_copy, r, pieces[0])
+            interleave_and_store(nc.scalar.copy, r, pieces[1])

@@ -25,7 +25,7 @@ GROUP_SIZES = ((1, 1, 1, 1, 2, 2, 2, 2, 2, 2), (2, 2, 2, 2, 2, 2, 2, 1, 1))
 LAG = 2
 LOADS_AHEAD = 4
 PE_COLUMNS = 200
-SCALAR_W1_COLUMNS = 32
+SCALAR_W1_COLUMNS = 48
 END_COLUMNS = 256
 BANK_COLUMNS = 256
 MATMUL_COLUMNS = 128

@@ -20,12 +20,12 @@ ROW_TILES = ROWS // P
 NETS = 2
 PASSES = HIDDEN // K_PASS
 VECTOR_RUN = 8
-SCALAR_RUN = 8
+SCALAR_RUN = 4
 GROUP_SIZES = ((1, 1, 1, 1, 2, 2, 2, 2, 2, 2), (2, 2, 2, 2, 2, 2, 2, 1, 1))
 LAG = 2
 LOADS_AHEAD = 4
-PE_COLUMNS = 200
-SCALAR_W1_COLUMNS = 48
+PE_COLUMNS = 204
+SCALAR_W1_COLUMNS = (0, 48, 80)
 END_COLUMNS = 256
 BANK_COLUMNS = 256
 MATMUL_COLUMNS = 128
@@ -127,7 +127,7 @@ def tile_affinecoupling_pa_k_kernel(
             x_grouped[j] = short.tile(
                 [P, x_columns(j), PACK], BF16, name="x_grouped", align_bytes=64
             )
-            by_scalar = steps_in(j) * SCALAR_W1_COLUMNS
+            by_scalar = SCALAR_W1_COLUMNS[steps_in(j)]
             if by_scalar > 0:
                 regroup(
                     nc.scalar.copy, SCALAR_RUN, x_grouped[j][:, 0:by_scalar, :], x_planes[j][:, :, 0:by_scalar]
@@ -136,7 +136,7 @@ def tile_affinecoupling_pa_k_kernel(
         def regroup_x(j):
             if x_columns(j) == 0:
                 return
-            part = slice(steps_in(j) * SCALAR_W1_COLUMNS, x_columns(j))
+            part = slice(SCALAR_W1_COLUMNS[steps_in(j)], x_columns(j))
             regroup(
                 nc.vector.tensor_copy,
                 VECTOR_RUN,

@@ -69,8 +69,8 @@ def tile_affinecoupling_pa_k_kernel(
         ctx.enter_context(tc.manual_schedule())
         const = ctx.enter_context(tc.tile_pool(name="const", bufs=1))
         raw = ctx.enter_context(tc.tile_pool(name="raw", bufs=LOADS_AHEAD))
-        short = ctx.enter_context(tc.tile_pool(name="short", bufs=2))
-        work = ctx.enter_context(tc.tile_pool(name="work", bufs=3))
+        short = ctx.enter_context(tc.tile_pool(name="short", bufs=3))
+        work = ctx.enter_context(tc.tile_pool(name="work", bufs=4))
         hidden_psum = ctx.enter_context(tc.psum_pool(name="hidden_psum", bufs=4))
         sum_psum = ctx.enter_context(tc.psum_pool(name="sum_psum", bufs=1))
         w2_psum = ctx.enter_context(tc.psum_pool(name="w2_psum", bufs=2))

from contextlib import ExitStack

import concourse.mybir as mybir
from concourse.masks import make_identity

F32 = mybir.dt.float32
BF16 = mybir.dt.bfloat16
U32 = mybir.dt.uint32
U8 = mybir.dt.uint8
FP8X4 = mybir.dt.float8_e4m3fn_x4
ACT = mybir.ActivationFunctionType
ALU = mybir.AluOpType

P = 128
PACK = 4
K_PASS = P * PACK
ROWS, FEATURES, HIDDEN = 256, 1024, 8192
HALF = FEATURES // 2
ROW_TILES = ROWS // P
NETS = 2
PASSES = HIDDEN // K_PASS
VECTOR_RUN = 8
SCALAR_RUN = 4
GROUP_SIZES = ((1, 1, 1, 1, 2, 2, 2, 2, 2, 2), (2, 2, 2, 2, 2, 2, 2, 1, 1))
LAG = 2
LOADS_AHEAD = 4
PE_COLUMNS = 204
SCALAR_W1_COLUMNS = (0, 48, 80)
END_COLUMNS = 256
BANK_COLUMNS = 256
MATMUL_COLUMNS = 128

FLOPS = 2 * ROWS * HALF * HIDDEN * 2 * NETS


def regroup(copy, run, grouped, planes):
    copy(
        out=grouped.rearrange("p (c i) t -> p c t i", i=run),
        in_=planes.rearrange("p t (c i) -> p c t i", i=run),
    )


def tile_affinecoupling_pa_k_kernel(
    tc, z, W1_s, b1_s, W2_s, b2_s, W1_t, b1_t, W2_t, b2_t, out_0, out_1
):
    nc = tc.nc
    w1_dram = (W1_s, W1_t)
    w2_dram = (W2_s, W2_t)

    groups = []
    for net in range(NETS):
        first = 0
        for size in GROUP_SIZES[net]:
            groups.append((net, first, size))
            first += size
    n_groups = len(groups)
    last_of_s = len(GROUP_SIZES[0]) - 1

    def steps_in(j):
        return groups[j][2] if 0 <= j < n_groups else 0

    def w1_columns(j):
        return K_PASS * steps_in(j)

    def x_columns(j):
        return w1_columns(j) + ROWS * steps_in(j - LAG)

    with ExitStack() as ctx:
        ctx.enter_context(tc.manual_schedule())
        const = ctx.enter_context(tc.tile_pool(name="const", bufs=1))
        raw = ctx.enter_context(tc.tile_pool(name="raw", bufs=LOADS_AHEAD))
        short = ctx.enter_context(tc.tile_pool(name="short", bufs=3))
        work = ctx.enter_context(tc.tile_pool(name="work", bufs=4))
        hidden_psum = ctx.enter_context(tc.psum_pool(name="hidden_psum", bufs=4))
        sum_psum = ctx.enter_context(tc.psum_pool(name="sum_psum", bufs=1))
        w2_psum = ctx.enter_context(tc.psum_pool(name="w2_psum", bufs=2))

        x_planes, w2_planes = {}, {}
        x_grouped, w2_grouped = {}, {}
        w1_mx, w2_mx, h_mx = {}, {}, {}
        h_banks, w2_banks = {}, {}
        second_biases = {}
        sums = {}

        def quantise(pool, grouped, columns, name):
            words = pool.tile([P, columns], U32, name=name + "_words", align_bytes=64)
            scales = pool.tile([P, columns], U8, name=name + "_scales", align_bytes=64)
            nc.vector.quantize_mx(
                out=words[:].bitcast(FP8X4),
                scales=scales[:],
                in_=grouped.rearrange("p c t -> p (c t)"),
            )
            return words, scales

        def h_pieces(j):
            return ROW_TILES if j == n_groups - 1 else 1


        def load_x(j):
            if x_columns(j) == 0:
                return
            x_planes[j] = raw.tile([P, PACK, x_columns(j)], BF16, name="x_planes")
            if steps_in(j) == 0:
                return
            net, first, size = groups[j]
            units = slice(first * K_PASS, (first + size) * K_PASS)
            nc.sync.dma_start(
                out=x_planes[j][:, :, 0 : w1_columns(j)],
                in_=w1_dram[net][:, units].rearrange("(t p) h -> p t h", p=P),
            )

        def load_w2(j):
            if steps_in(j) == 0:
                return
            net, first, size = groups[j]
            w2_planes[j] = raw.tile([P, PACK, size * HALF], BF16, name="w2_planes")
            for g in range(size):
                units = slice((first + g) * K_PASS, (first + g + 1) * K_PASS)
                nc.sync.dma_start(
                    out=w2_planes[j][:, :, g * HALF : (g + 1) * HALF],
                    in_=w2_dram[net][units, :].rearrange("(t p) n -> p t n", p=P),
                )

        def regroup_x_by_scalar(j):
            if x_columns(j) == 0:
                return
            x_grouped[j] = short.tile(
                [P, x_columns(j), PACK], BF16, name="x_grouped", align_bytes=64
            )
            by_scalar = SCALAR_W1_COLUMNS[steps_in(j)]
            if by_scalar > 0:
                regroup(
                    nc.scalar.copy, SCALAR_RUN, x_grouped[j][:, 0:by_scalar, :], x_planes[j][:, :, 0:by_scalar]
                )

        def regroup_x(j):
            if x_columns(j) == 0:
                return
            part = slice(SCALAR_W1_COLUMNS[steps_in(j)], x_columns(j))
            regroup(
                nc.vector.tensor_copy,
                VECTOR_RUN,
                x_grouped[j][:, part, :],
                x_planes[j][:, :, part],
            )

        def last_hidden():
            j = n_groups - 1
            columns = steps_in(j) * ROWS
            words = short.tile([P, columns], U32, name="h_words", align_bytes=64)
            scales = short.tile([P, columns], U8, name="h_scales", align_bytes=64)
            for r in range(ROW_TILES):
                part = slice(r * P, (r + 1) * P)
                regroup(
                    nc.vector.tensor_copy,
                    VECTOR_RUN,
                    x_grouped[j + LAG][:, part, :],
                    x_planes[j + LAG][:, :, part],
                )
                nc.vector.quantize_mx(
                    out=words[:, part].bitcast(FP8X4),
                    scales=scales[:, part],
                    in_=x_grouped[j + LAG][:, part, :].rearrange("p c t -> p (c t)"),
                )
            h_mx[j] = (words, scales)

        def regroup_w2(j):
            if steps_in(j) == 0:
                return
            w2_grouped[j] = work.tile(
                [P, steps_in(j) * HALF, PACK], BF16, name="w2_grouped", align_bytes=64
            )
            by_tensor = steps_in(j) * PE_COLUMNS
            regroup(
                nc.scalar.copy, SCALAR_RUN, w2_grouped[j][:, by_tensor:, :], w2_planes[j][:, :, by_tensor:]
            )
            for b, bank in enumerate(w2_banks[j]):
                columns = slice(b * BANK_COLUMNS, min((b + 1) * BANK_COLUMNS, by_tensor))
                nc.scalar.copy(
                    out=w2_grouped[j][:, columns, :],
                    in_=bank[:, 0 : columns.stop - columns.start, :],
                )

        def regroup_w2_by_tensor(j):
            if steps_in(j) == 0:
                return
            by_tensor = steps_in(j) * PE_COLUMNS
            w2_banks[j] = []
            for bank_start in range(0, by_tensor, BANK_COLUMNS):
                bank = w2_psum.tile([P, BANK_COLUMNS, PACK], BF16, name="w2_bank")
                w2_banks[j].append(bank)
                bank_stop = min(bank_start + BANK_COLUMNS, by_tensor)
                for start in range(bank_start, bank_stop, MATMUL_COLUMNS):
                    stop = min(start + MATMUL_COLUMNS, bank_stop)
                    nc.tensor.matmul(
                        out=bank[:, start - bank_start : stop - bank_start, :],
                        lhsT=identity_bf16[:],
                        rhs=w2_planes[j][:, :, start:stop].rearrange("p t c -> p c t"),
                        start=True,
                        stop=True,
                    )

        def quantise_w1(j):
            if steps_in(j) == 0:
                return
            w1_mx[j] = quantise(short, x_grouped[j][:, 0 : w1_columns(j), :], w1_columns(j), "w1")

        def quantise_w2(j):
            if steps_in(j) == 0:
                return
            w2_mx[j] = quantise(work, w2_grouped[j][:], steps_in(j) * HALF, "w2")

        def first_matmul(j):
            if steps_in(j) == 0:
                return
            words, scales = w1_mx[j]
            h_banks[j] = []
            for half_step in range(steps_in(j) * PACK // 2):
                bank = hidden_psum.tile([P, 2, ROWS], F32, name="h_bank")
                h_banks[j].append(bank)
                for i in range(2):
                    units = slice((2 * half_step + i) * P, (2 * half_step + i + 1) * P)
                    nc.tensor.matmul_mx(
                        out=bank[:, i, :],
                        lhsT=words[:, units].bitcast(FP8X4),
                        lhsT_scale=scales[:, units],
                        rhs=a_words[:].bitcast(FP8X4),
                        rhs_scale=a_scales[:],
                        start=True,
                        stop=True,
                    )

        def bias_relu(j):
            if steps_in(j) == 0:
                return
            net, first, size = groups[j]
            for g in range(size):
                rows = slice(
                    w1_columns(j + LAG) + g * ROWS, w1_columns(j + LAG) + (g + 1) * ROWS
                )
                width = ROWS // h_pieces(j)
                for start in range(0, ROWS, width):
                    for t in range(PACK):
                        tile_index = g * PACK + t
                        bias_column = (net * PASSES + first) * PACK + tile_index
                        nc.scalar.activation(
                            out=x_planes[j + LAG][:, t, rows.start + start : rows.start + start + width],
                            in_=h_banks[j][tile_index // 2][:, tile_index % 2, start : start + width],
                            func=ACT.Relu,
                            bias=b1_columns[:, bias_column : bias_column + 1],
                            scale=1.0,
                        )

        def quantise_h(j):
            if steps_in(j) == 0:
                return
            h_mx[j] = quantise(
                short,
                x_grouped[j + LAG][:, w1_columns(j + LAG) :, :],
                steps_in(j) * ROWS,
                "h",
            )

        def second_matmul(j):
            if steps_in(j) == 0:
                return
            net, first, size = groups[j]
            if first == 0:
                sums[net] = [
                    sum_psum.tile([P, HALF], F32, name="sum%d" % r) for r in range(ROW_TILES)
                ]
            h_words, h_scales = h_mx[j]
            w_words, w_scales = w2_mx[j]
            for r in range(ROW_TILES):
                for g in range(size):
                    rows = slice(g * ROWS + r * P, g * ROWS + (r + 1) * P)
                    columns = slice(g * HALF, (g + 1) * HALF)
                    nc.tensor.matmul_mx(
                        out=sums[net][r][:],
                        lhsT=h_words[:, rows].bitcast(FP8X4),
                        lhsT_scale=h_scales[:, rows],
                        rhs=w_words[:, columns].bitcast(FP8X4),
                        rhs_scale=w_scales[:, columns],
                        start=(first + g == 0),
                        stop=(first + g == PASSES - 1),
                    )


        def s_bias_and_row_sum(r):
            nc.vector.scalar_tensor_tensor(
                out=s_sb[:, r, :],
                in0=sums[0][r][:],
                scalar=1.0,
                in1=second_biases["s"][:],
                op0=ALU.mult,
                op1=ALU.add,
                accum_out=logdet_columns[:, r : r + 1],
            )

        def s_exp(r):
            nc.scalar.activation(out=shift[:, r, :], in_=s_sb[:, r, :], func=ACT.Exp)

        def s_times_b(r):
            nc.vector.tensor_tensor(
                out=shift[:, r, :], in0=shift[:, r, :], in1=z_pairs[:, r, :, 1], op=ALU.mult
            )

        def s_plus_bias(r):
            nc.vector.tensor_tensor(
                out=shift[:, r, :], in0=shift[:, r, :], in1=second_biases["t"][:], op=ALU.add
            )

        def logdet_transpose():
            logdet_psum = hidden_psum.tile([P, P], F32, name="logdet_psum", tag="h_bank")
            sums["logdet"] = logdet_psum
            nc.tensor.transpose(out=logdet_psum[:], in_=logdet_columns[:], identity=identity_f32[:])

        def load_second_biases():
            for net_name, bias in (("s", b2_s), ("t", b2_t)):
                second_biases[net_name] = const.tile([P, HALF], BF16, name="b2_" + net_name)
                nc.sync.dma_start(out=second_biases[net_name][:], in_=bias.partition_broadcast(P))


        z_sb = const.tile([P, ROW_TILES, FEATURES], BF16)
        b1_rows = const.tile([P, P], BF16)
        load_x(0)
        nc.sync.dma_start(out=z_sb[:], in_=z.rearrange("(r p) d -> p r d", p=P))
        nc.sync.dma_start(out=b1_rows[0 : P // 2, :], in_=b1_s.rearrange("(i c) -> i c", c=P))
        nc.sync.dma_start(out=b1_rows[P // 2 : P, :], in_=b1_t.rearrange("(i c) -> i c", c=P))
        load_w2(0)
        for j in range(1, LOADS_AHEAD):
            load_x(j)
            load_w2(j)

        identity_bf16 = const.tile([P, P], BF16)
        identity_f32 = const.tile([P, P], F32)
        make_identity(nc, identity_bf16[:])
        make_identity(nc, identity_f32[:])

        table_in = const.tile([P, 1], F32)
        table_out = const.tile([P, 1], F32)
        nc.vector.memset(table_in[:], 0.0)
        nc.scalar.activation(out=table_out[:], in_=table_in[:], func=ACT.Exp)

        logdet_columns = const.tile([P, P], F32)
        logdet_rows = const.tile([P, P], F32)
        nc.vector.memset(logdet_columns[:], 0.0)
        s_sb = const.tile([P, ROW_TILES, HALF], F32)
        shift = const.tile([P, ROW_TILES, HALF], F32)
        z_out_planes = const.tile([P, ROW_TILES, 2, HALF], F32)
        z_out_sb = const.tile([P, ROW_TILES, FEATURES], F32)
        z_pairs = z_sb[:].rearrange("p r (k e) -> p r k e", e=2)
        a_grouped = const.tile([P, ROWS, PACK], BF16, align_bytes=64)
        b1_columns = const.tile([P, P], F32)
        a_words = const.tile([P, ROWS], U32, align_bytes=64)
        a_scales = const.tile([P, ROWS], U8, align_bytes=64)

        a_psum = hidden_psum.tile([P, ROW_TILES, PACK, P], BF16, name="a_psum", tag="h_bank")
        for r in range(ROW_TILES):
            for t in range(PACK):
                nc.tensor.transpose(
                    out=a_psum[:, r, t, :],
                    in_=z_pairs[:, r, t * P : (t + 1) * P, 0],
                    identity=identity_bf16[:],
                )
        b1_psum = hidden_psum.tile([P, P], BF16, name="b1_psum", tag="h_bank")
        nc.tensor.transpose(out=b1_psum[:], in_=b1_rows[:], identity=identity_bf16[:])

        def quantise_a_and_copy_b1():
            nc.vector.tensor_copy(
                out=a_grouped[:].rearrange("p (r i) t -> p r i t", r=ROW_TILES),
                in_=a_psum[:].rearrange("p r t i -> p r i t"),
            )
            nc.vector.tensor_copy(out=b1_columns[:], in_=b1_psum[:])
            nc.vector.quantize_mx(
                out=a_words[:].bitcast(FP8X4),
                scales=a_scales[:],
                in_=a_grouped[:].rearrange("p c t -> p (c t)"),
            )

        regroup_w2_by_tensor(0)
        regroup_x_by_scalar(0)
        nc.scalar.copy(out=z_out_planes[:, :, 0, :], in_=z_pairs[:, :, :, 0])

        for tick in range(-LAG, n_groups):
            since_s = tick - last_of_s
            bias_relu(tick + 1)
            if since_s == 3:
                logdet_transpose()
            regroup_w2(tick + 2)
            if since_s == 3:
                nc.scalar.copy(out=logdet_rows[:], in_=sums["logdet"][:])
            regroup_x_by_scalar(tick + 3)
            if tick < n_groups - 1:
                regroup_x(tick + 2)
            quantise_w2(tick + 1)
            if since_s == 1:
                for r in range(ROW_TILES):
                    s_bias_and_row_sum(r)
            quantise_w1(tick + 2)
            if tick == -LAG:
                quantise_a_and_copy_b1()
            first_matmul(tick + 2)
            if tick < n_groups - 1:
                quantise_h(tick)
            else:
                last_hidden()
            second_matmul(tick)
            regroup_w2_by_tensor(tick + 3)
            for r in range(ROW_TILES):
                if since_s == 2 + r:
                    s_exp(r)
                if since_s == 3 + r:
                    s_times_b(r)
                if since_s == 5 + r:
                    s_plus_bias(r)
            if tick == last_of_s - 3:
                load_second_biases()
            load_x(tick + 2 + LOADS_AHEAD)
            load_w2(tick + 2 + LOADS_AHEAD)

        nc.sync.dma_start(
            out=out_1.rearrange("(r i) -> r i", r=ROW_TILES), in_=logdet_rows[0:ROW_TILES, :]
        )
        pieces = [slice(k, k + END_COLUMNS) for k in range(0, HALF, END_COLUMNS)]

        def add(r, piece):
            nc.vector.tensor_tensor(
                out=z_out_planes[:, r, 1, piece],
                in0=sums[1][r][:, piece],
                in1=shift[:, r, piece],
                op=ALU.add,
            )

        def interleave_and_store(copy, r, piece):
            features = slice(2 * piece.start, 2 * piece.stop)
            copy(
                out=z_out_sb[:, r, features].rearrange("p (k e) -> p k e", e=2),
                in_=z_out_planes[:, r, :, piece].rearrange("p e k -> p k e"),
            )
            nc.sync.dma_start(
                out=out_0[r * P : (r + 1) * P, features], in_=z_out_sb[:, r, features]
            )

        for r in range(ROW_TILES):
            for piece in pieces:
                add(r, piece)
            interleave_and_store(nc.vector.tensor_copy, r, pieces[0])
            interleave_and_store(nc.scalar.copy, r, pieces[1])
